import numpy as np
import ml_dtypes


def mxq(x, axis, fmt="e4m3"):
    dtype, down = {"e4m3": (ml_dtypes.float8_e4m3fn, 7), "e5m2": (ml_dtypes.float8_e5m2, 14)}[fmt]
    v = np.moveaxis(np.asarray(x, np.float32).astype(ml_dtypes.bfloat16).astype(np.float64), axis, -1)
    blocks = v.reshape(v.shape[:-1] + (-1, 32))
    amax = np.abs(blocks).max(-1, keepdims=True)
    byte = np.maximum(np.where(amax > 0, np.frexp(amax)[1] - 1 + 127, 0) - down, 1)
    scale = np.exp2(byte - 127.0)
    codes = (blocks / scale).astype(np.float32).astype(dtype).astype(np.float64)
    return np.moveaxis((codes * scale).reshape(v.shape), -1, axis)


WIDE = False


def mx_kscale(k):
    if not WIDE:
        return np.ones(k)
    levels = np.array([10, -10, 5, -5, 0])
    if k % 512:
        return np.exp2(np.random.permutation(np.resize(levels, k // 32))).repeat(32)
    a = np.empty((k // 512, 16))
    for p in range(k // 512):
        a[p, :8] = np.random.permutation(np.resize(levels, 8))
        for g in range(8):
            far = levels[np.abs(levels - a[p, g]) >= 10]
            a[p, g + 8] = far[np.random.randint(len(far))]
    return np.exp2(a.ravel()).repeat(32)


BF16 = ml_dtypes.bfloat16


def bf(x):
    return np.asarray(x, np.float32).astype(BF16)


def f64(x):
    return np.asarray(x).astype(np.float64)


B, S, D, F, P, NQ = 2, 128, 1024, 1024, 1024, 3
LN_EPS = 1e-5


def layernorm(v, g, b):
    m = v.mean(-1, keepdims=True)
    var = v.var(-1, keepdims=True)
    return (v - m) / np.sqrt(var + LN_EPS) * g + b


def setup_inputs():
    s = mx_kscale(P)
    return {"in_proto": bf(np.random.standard_normal((NQ, F, P)) * s),
            "pt_w": bf(np.random.standard_normal((NQ, D, P)) / np.sqrt(P) / s),
            "pln_g": bf(1.0 + 0.1 * np.random.standard_normal((NQ, D))),
            "pln_b": bf(0.1 * np.random.standard_normal((NQ, D))),
            "proto_w": bf(np.random.standard_normal((NQ, F, D)) * 0.5)}


def core(in_proto, pt_w, pln_g, pln_b, proto_w):
    prc = mxq(f64(in_proto), 2, "e4m3") @ mxq(f64(pt_w), 2, "e4m3").transpose(0, 2, 1)
    return f64(proto_w) + layernorm(prc, f64(pln_g)[:, None, :], f64(pln_b)[:, None, :])


def e4m3fn_bytes(y):
    return np.clip(np.asarray(y, np.float64), -448.0, 448.0).astype(np.float32).astype(ml_dtypes.float8_e4m3fn).view(np.uint8)


Y_SCALE = 190.0


def reference(in_proto, pt_w, pln_g, pln_b, proto_w):
    out = core(in_proto, pt_w, pln_g, pln_b, proto_w)
    return out, e4m3fn_bytes(out * Y_SCALE)

@@ -1,0 +1,312 @@
+from contextlib import ExitStack
+
+import concourse.mybir as mybir
+from concourse.masks import make_identity
+
+FLOPS = 2 * 3 * 1024 * 1024 * 1024
+
+F32 = mybir.dt.float32
+BF16 = mybir.dt.bfloat16
+U32 = mybir.dt.uint32
+U8 = mybir.dt.uint8
+FP8X4 = mybir.dt.float8_e4m3fn_x4
+FP8 = mybir.dt.float8_e4m3fn
+ACT = mybir.ActivationFunctionType
+ALU = mybir.AluOpType
+
+P = 128
+NB = 3
+RT = 8
+NT = NB * RT
+K = 1024
+D = 1024
+HALF = 512
+LN_EPS = 1e-5
+Y_SCALE = 190.0
+AHEAD = 6
+FIRST = -9
+HEAD_W = 8
+
+
+def tile_moietransformerblock_pb_kernel(tc, in_proto, pt_w, pln_g, pln_b, proto_w, out_0, out_1):
+    nc = tc.nc
+    a_view = [in_proto[n].rearrange("(p t) k -> p t k", t=RT) for n in range(NB)]
+    w_view = [pt_w[n].rearrange("(t p) k -> p t k", p=P) for n in range(NB)]
+    r_view = [proto_w[n].rearrange("(p t) d -> p t d", t=RT) for n in range(NB)]
+    o0_view = [out_0[n].rearrange("(p t) d -> p t d", t=RT) for n in range(NB)]
+    o1_view = [out_1[n].rearrange("(p t) d -> p t d", t=RT) for n in range(NB)]
+
+    with ExitStack() as ctx:
+        const = ctx.enter_context(tc.tile_pool(name="const", bufs=1))
+        raw = ctx.enter_context(tc.tile_pool(name="raw", bufs=6))
+        grp = ctx.enter_context(tc.tile_pool(name="grp", bufs=3))
+        acode = ctx.enter_context(tc.tile_pool(name="acode", bufs=4))
+        wcode = ctx.enter_context(tc.tile_pool(name="wcode", bufs=2))
+        small = ctx.enter_context(tc.tile_pool(name="small", bufs=4))
+        tpool = ctx.enter_context(tc.tile_pool(name="tpool", bufs=2))
+        cpool = ctx.enter_context(tc.tile_pool(name="cpool", bufs=3))
+        ypool = ctx.enter_context(tc.tile_pool(name="ypool", bufs=4))
+        opool = ctx.enter_context(tc.tile_pool(name="opool", bufs=2))
+        xps = ctx.enter_context(tc.psum_pool(name="xps", bufs=2))
+        tps = ctx.enter_context(tc.psum_pool(name="tps", bufs=4))
+
+        ident = const.tile([P, P], F32, name="ident")
+        make_identity(nc, ident[:])
+        eps = const.tile([P, 1], F32, name="eps")
+        nc.vector.memset(eps[:], LN_EPS)
+        warm = const.tile([P, 1], F32, name="warm")
+        nc.scalar.activation(out=warm[:], in_=eps[:], func=ACT.Sqrt, bias=eps[:], scale=1.0)
+        st = [const.tile([P, 9], F32, name="st%d" % j) for j in range(2)]
+        for j in range(2):
+            nc.vector.memset(st[j][:, 6:7], float(HALF))
+        gain = const.tile([P, NB, D], BF16, name="gain")
+        beta = const.tile([P, NB, D], BF16, name="beta")
+
+        wraw = {}
+        araw = {}
+        rraw = {}
+        tp_a = {}
+        tp_w = {}
+        g_a = {}
+        g_w = {}
+        a_c = {}
+        a_s = {}
+        w_c = {}
+        w_s = {}
+        x_ps = {}
+        sums = {}
+        mv = {}
+        sd = {}
+        rs = {}
+        t_sb = {}
+        c_sb = {}
+        y_sb = {}
+        o_sb = {}
+
+        loads = []
+        for k in range(NT // 2):
+            loads.append((2 * k - 9, 0, "w", k))
+            loads.append((2 * k - 3, 1, "a", k))
+            loads.append((2 * k - 1, 2, "r", k))
+        for n in range(NB):
+            loads.append((RT * n - 1, 3, "b", n))
+            loads.append((RT * n, 4, "g", n))
+        loads = sorted(loads)
+
+        def issue_load(kind, k):
+            n = k // 4
+            c = k % 4
+            if kind == "w":
+                wr = raw.tile([P, 2, K], BF16, name="wr", tag="wr")
+                nc.sync.dma_start(out=wr[:], in_=w_view[n][:, 2 * c : 2 * c + 2, :])
+                wraw[k] = wr
+            elif kind == "a":
+                ar = raw.tile([P, 2, K], BF16, name="ar", tag="ar")
+                nc.sync.dma_start(out=ar[:], in_=a_view[n][:, 2 * c : 2 * c + 2, :])
+                araw[k] = ar
+            elif kind == "r":
+                rr = raw.tile([P, 2, D], BF16, name="rr", tag="rr")
+                nc.sync.dma_start(out=rr[:], in_=r_view[n][:, 2 * c : 2 * c + 2, :])
+                rraw[k] = rr
+            elif kind == "b":
+                nc.sync.dma_start(out=beta[:, k, :], in_=pln_b[k].partition_broadcast(P))
+            else:
+                nc.sync.dma_start(out=gain[:, k, :], in_=pln_g[k].partition_broadcast(P))
+
+        def transposes(src, dst):
+            words = src.bitcast(F32)
+            for g in range(2):
+                for u in range(2):
+                    q = 2 * g + u
+                    nc.tensor.transpose(
+                        out=dst[:, q * P : (q + 1) * P],
+                        in_=words[:, 256 * g + u : 256 * (g + 1) : 2],
+                        identity=ident[:],
+                    )
+
+        def transpose_a(i):
+            tp = tps.tile([P, HALF], F32, name="tp", tag="tp")
+            transposes(araw[i // 2][:, i % 2, :], tp)
+            tp_a[i] = tp
+
+        def transpose_w(w):
+            tp = tps.tile([P, HALF], F32, name="tp", tag="tp")
+            transposes(wraw[w // 2][:, w % 2, :], tp)
+            tp_w[w] = tp
+
+        def interleave(on_vector, tp, gt):
+            dst = gt[:].bitcast(F32).rearrange("p (g r u) -> p g r u", g=2, u=2)
+            src = tp[:].rearrange("p (g u r) -> p g r u", g=2, u=2)
+            if on_vector:
+                nc.vector.tensor_copy(out=dst, in_=src)
+            else:
+                nc.scalar.copy(out=dst, in_=src)
+
+        def copy_a(i):
+            ga = grp.tile([P, K], BF16, name="ga", tag="ga", align_bytes=64)
+            interleave(False, tp_a[i], ga)
+            g_a[i] = ga
+
+        def copy_w(w):
+            gw = grp.tile([P, K], BF16, name="gw", tag="gw", align_bytes=64)
+            interleave(w < HEAD_W and w % 2 == 1, tp_w[w], gw)
+            g_w[w] = gw
+
+        def quant_a(i):
+            ac = acode.tile([P, 2 * P], U32, name="ac", tag="ac", align_bytes=64)
+            asc = acode.tile([P, 2 * P], U8, name="asc", tag="asc", align_bytes=64)
+            nc.vector.quantize_mx(out=ac[:].bitcast(FP8X4), scales=asc[:], in_=g_a[i][:])
+            a_c[i] = ac
+            a_s[i] = asc
+
+        def quant_w(w):
+            n = w // RT
+            j = w % RT
+            if j == 0:
+                wc = wcode.tile([P, 2, D], U32, name="wc", tag="wc", align_bytes=64)
+                wsc = wcode.tile([P, 2, D], U8, name="wsc", tag="wsc", align_bytes=64)
+                w_c[n] = wc
+                w_s[n] = wsc
+            for g in range(2):
+                nc.vector.quantize_mx(
+                    out=w_c[n][:, g, j * P : (j + 1) * P].bitcast(FP8X4),
+                    scales=w_s[n][:, g, j * P : (j + 1) * P],
+                    in_=g_w[w][:, g * HALF : (g + 1) * HALF],
+                )
+
+        def matmuls(i):
+            n = i // RT
+            x0 = xps.tile([P, HALF], F32, name="x0", tag="x0")
+            x1 = xps.tile([P, HALF], F32, name="x1", tag="x1")
+            x_ps[i] = (x0, x1)
+            for g in range(2):
+                for h in range(2):
+                    nc.tensor.matmul_mx(
+                        out=x_ps[i][h][:],
+                        lhsT=a_c[i][:, g * P : (g + 1) * P].bitcast(FP8X4),
+                        lhsT_scale=a_s[i][:, g * P : (g + 1) * P],
+                        rhs=w_c[n][:, g, h * HALF : (h + 1) * HALF].bitcast(FP8X4),
+                        rhs_scale=w_s[n][:, g, h * HALF : (h + 1) * HALF],
+                        start=(g == 0),
+                        stop=(g == 1),
+                    )
+
+        def row_sum(i):
+            sm = small.tile([P, 1], F32, name="sm", tag="sm")
+            junk = small.tile([P, HALF], BF16, name="junk", tag="junk")
+            nc.scalar.activation(out=junk[:], in_=x_ps[i][1][:], func=ACT.Copy, accum_out=sm[:])
+            sums[i] = sm
+
+        def half_mean(i):
+            nc.scalar.activation(out=st[i % 2][:, 7:8], in_=sums[i][:], func=ACT.Copy, scale=1.0 / HALF)
+
+        def half_m2(i):
+            junk = small.tile([P, HALF], BF16, name="junk", tag="junk")
+            nc.scalar.activation(
+                out=junk[:], in_=x_ps[i][1][:], func=ACT.Square, scale=-1.0,
+                bias=st[i % 2][:, 7:8], accum_out=st[i % 2][:, 8:9],
+            )
+
+        def bn(i):
+            nc.vector.bn_stats(out=st[i % 2][:, 0:6], in_=x_ps[i][0][:])
+
+        def aggr(i):
+            m = small.tile([P, 2], F32, name="m", tag="m")
+            nc.vector.bn_aggr(out=m[:], in_=st[i % 2][:])
+            mv[i] = m
+
+        def std(i):
+            sdev = small.tile([P, 1], F32, name="sdev", tag="sdev")
+            nc.scalar.activation(out=sdev[:], in_=mv[i][:, 1:2], func=ACT.Sqrt, bias=eps[:], scale=1.0)
+            sd[i] = sdev
+
+        def rstd(i):
+            r = small.tile([P, 1], F32, name="r", tag="r")
+            nc.vector.reciprocal(out=r[:], in_=sd[i][:])
+            rs[i] = r
+
+        def centre_gain(i):
+            n = i // RT
+            t = tpool.tile([P, D], F32, name="t", tag="t")
+            for h in range(2):
+                nc.vector.scalar_tensor_tensor(
+                    out=t[:, h * HALF : (h + 1) * HALF], in0=x_ps[i][h][:], scalar=mv[i][:, 0:1],
+                    in1=gain[:, n, h * HALF : (h + 1) * HALF], op0=ALU.subtract, op1=ALU.mult,
+                )
+            t_sb[i] = t
+
+        def resid(i):
+            n = i // RT
+            c = cpool.tile([P, D], F32, name="c", tag="c")
+            for h in range(2):
+                nc.gpsimd.tensor_tensor(
+                    out=c[:, h * HALF : (h + 1) * HALF], in0=rraw[i // 2][:, i % 2, h * HALF : (h + 1) * HALF],
+                    in1=beta[:, n, h * HALF : (h + 1) * HALF], op=ALU.add,
+                )
+            c_sb[i] = c
+
+        def scale_add(i):
+            y = ypool.tile([P, D], F32, name="y", tag="y")
+            nc.vector.scalar_tensor_tensor(
+                out=y[:], in0=t_sb[i][:], scalar=rs[i][:], in1=c_sb[i][:], op0=ALU.mult, op1=ALU.add,
+            )
+            nc.sync.dma_start(out=o0_view[i // RT][:, i % RT, :], in_=y[:])
+            y_sb[i] = y
+
+        def cast(i):
+            q = i % 4
+            if q == 0:
+                o8 = opool.tile([P, 4, D], FP8, name="o8", tag="o8")
+                o_sb[i // 4] = o8
+            o = o_sb[i // 4]
+            nc.scalar.activation(out=o[:, q, :], in_=y_sb[i][:], func=ACT.Copy, scale=Y_SCALE, saturate=False)
+            if q == 3:
+                t0 = (i % RT) - 3
+                nc.sync.dma_start(out=o1_view[i // RT][:, t0 : t0 + 4, :], in_=o[:].bitcast(U8))
+
+        def ok(i):
+            return 0 <= i < NT
+
+        with tc.manual_schedule():
+            for s in range(FIRST, NT + 1):
+                for need, order, kind, k in loads:
+                    if need - AHEAD == s or (s == FIRST and need - AHEAD < FIRST):
+                        issue_load(kind, k)
+                i1 = s + 1
+                ia = s + 3
+                iw = s + 9
+                if ok(i1):
+                    matmuls(i1)
+                if ok(ia):
+                    transpose_a(ia)
+                if ok(iw):
+                    transpose_w(iw)
+                if ok(s):
+                    std(s)
+                if ok(i1):
+                    row_sum(i1)
+                if ok(s - 1):
+                    scale_add(s - 1)
+                if ok(ia):
+                    copy_a(ia)
+                if ok(i1):
+                    half_mean(i1)
+                if ok(iw):
+                    copy_w(iw)
+                if ok(i1):
+                    half_m2(i1)
+                if ok(s):
+                    centre_gain(s)
+                    rstd(s)
+                if ok(i1):
+                    bn(i1)
+                if ok(ia):
+                    quant_a(ia)
+                if ok(iw):
+                    quant_w(iw)
+                if ok(i1):
+                    aggr(i1)
+                if ok(s - 1):
+                    cast(s - 1)
+                if ok(i1):
+                    resid(i1)

@@ -24,7 +24,8 @@ HALF = 512
 LN_EPS = 1e-5
 Y_SCALE = 190.0
 AHEAD = 6
-FIRST = -9
+FIRST = -11
+N_WARM = 8
 HEAD_W = 8
 
 
@@ -59,6 +60,8 @@ def tile_moietransformerblock_pb_kernel(tc, in_proto, pt_w, pln_g, pln_b, proto_
         st = [const.tile([P, 9], F32, name="st%d" % j) for j in range(2)]
         for j in range(2):
             nc.vector.memset(st[j][:, 6:7], float(HALF))
+        zeros = const.tile([P, HALF], BF16, name="zeros")
+        nc.vector.memset(zeros[:], 0.0)
         gain = const.tile([P, NB, D], BF16, name="gain")
         beta = const.tile([P, NB, D], BF16, name="beta")
 
@@ -85,8 +88,8 @@ def tile_moietransformerblock_pb_kernel(tc, in_proto, pt_w, pln_g, pln_b, proto_
 
         loads = []
         for k in range(NT // 2):
-            loads.append((2 * k - 9, 0, "w", k))
-            loads.append((2 * k - 3, 1, "a", k))
+            loads.append((2 * k - 11, 0, "w", k))
+            loads.append((2 * k - 4, 1, "a", k))
             loads.append((2 * k - 1, 2, "r", k))
         for n in range(NB):
             loads.append((RT * n - 1, 3, "b", n))
@@ -174,27 +177,28 @@ def tile_moietransformerblock_pb_kernel(tc, in_proto, pt_w, pln_g, pln_b, proto_
                     in_=g_w[w][:, g * HALF : (g + 1) * HALF],
                 )
 
-        def matmuls(i):
+        def matmuls(i, h):
             n = i // RT
-            x0 = xps.tile([P, HALF], F32, name="x0", tag="x0")
-            x1 = xps.tile([P, HALF], F32, name="x1", tag="x1")
-            x_ps[i] = (x0, x1)
+            x = xps.tile([P, HALF], F32, name="x%d" % h, tag="x%d" % h)
+            x_ps[(i, h)] = x
             for g in range(2):
-                for h in range(2):
-                    nc.tensor.matmul_mx(
-                        out=x_ps[i][h][:],
-                        lhsT=a_c[i][:, g * P : (g + 1) * P].bitcast(FP8X4),
-                        lhsT_scale=a_s[i][:, g * P : (g + 1) * P],
-                        rhs=w_c[n][:, g, h * HALF : (h + 1) * HALF].bitcast(FP8X4),
-                        rhs_scale=w_s[n][:, g, h * HALF : (h + 1) * HALF],
-                        start=(g == 0),
-                        stop=(g == 1),
-                    )
+                nc.tensor.matmul_mx(
+                    out=x[:],
+                    lhsT=a_c[i][:, g * P : (g + 1) * P].bitcast(FP8X4),
+                    lhsT_scale=a_s[i][:, g * P : (g + 1) * P],
+                    rhs=w_c[n][:, g, h * HALF : (h + 1) * HALF].bitcast(FP8X4),
+                    rhs_scale=w_s[n][:, g, h * HALF : (h + 1) * HALF],
+                    start=(g == 0),
+                    stop=(g == 1),
+                )
+
+        def dummy():
+            nc.tensor.matmul(out=warm_ps[:], lhsT=zeros[:, 0:P], rhs=zeros[:], start=True, stop=True)
 
         def row_sum(i):
             sm = small.tile([P, 1], F32, name="sm", tag="sm")
             junk = small.tile([P, HALF], BF16, name="junk", tag="junk")
-            nc.scalar.activation(out=junk[:], in_=x_ps[i][1][:], func=ACT.Copy, accum_out=sm[:])
+            nc.scalar.activation(out=junk[:], in_=x_ps[(i, 1)][:], func=ACT.Copy, accum_out=sm[:])
             sums[i] = sm
 
         def half_mean(i):
@@ -203,12 +207,12 @@ def tile_moietransformerblock_pb_kernel(tc, in_proto, pt_w, pln_g, pln_b, proto_
         def half_m2(i):
             junk = small.tile([P, HALF], BF16, name="junk", tag="junk")
             nc.scalar.activation(
-                out=junk[:], in_=x_ps[i][1][:], func=ACT.Square, scale=-1.0,
+                out=junk[:], in_=x_ps[(i, 1)][:], func=ACT.Square, scale=-1.0,
                 bias=st[i % 2][:, 7:8], accum_out=st[i % 2][:, 8:9],
             )
 
         def bn(i):
-            nc.vector.bn_stats(out=st[i % 2][:, 0:6], in_=x_ps[i][0][:])
+            nc.vector.bn_stats(out=st[i % 2][:, 0:6], in_=x_ps[(i, 0)][:])
 
         def aggr(i):
             m = small.tile([P, 2], F32, name="m", tag="m")
@@ -225,15 +229,15 @@ def tile_moietransformerblock_pb_kernel(tc, in_proto, pt_w, pln_g, pln_b, proto_
             nc.vector.reciprocal(out=r[:], in_=sd[i][:])
             rs[i] = r
 
-        def centre_gain(i):
+        def centre_gain(i, h):
             n = i // RT
-            t = tpool.tile([P, D], F32, name="t", tag="t")
-            for h in range(2):
-                nc.vector.scalar_tensor_tensor(
-                    out=t[:, h * HALF : (h + 1) * HALF], in0=x_ps[i][h][:], scalar=mv[i][:, 0:1],
-                    in1=gain[:, n, h * HALF : (h + 1) * HALF], op0=ALU.subtract, op1=ALU.mult,
-                )
-            t_sb[i] = t
+            if h == 1:
+                t = tpool.tile([P, D], F32, name="t", tag="t")
+                t_sb[i] = t
+            nc.vector.scalar_tensor_tensor(
+                out=t_sb[i][:, h * HALF : (h + 1) * HALF], in0=x_ps[(i, h)][:], scalar=mv[i][:, 0:1],
+                in1=gain[:, n, h * HALF : (h + 1) * HALF], op0=ALU.subtract, op1=ALU.mult,
+            )
 
         def resid(i):
             n = i // RT
@@ -247,9 +251,11 @@ def tile_moietransformerblock_pb_kernel(tc, in_proto, pt_w, pln_g, pln_b, proto_
 
         def scale_add(i):
             y = ypool.tile([P, D], F32, name="y", tag="y")
-            nc.vector.scalar_tensor_tensor(
-                out=y[:], in0=t_sb[i][:], scalar=rs[i][:], in1=c_sb[i][:], op0=ALU.mult, op1=ALU.add,
-            )
+            for h in (1, 0):
+                nc.vector.scalar_tensor_tensor(
+                    out=y[:, h * HALF : (h + 1) * HALF], in0=t_sb[i][:, h * HALF : (h + 1) * HALF], scalar=rs[i][:],
+                    in1=c_sb[i][:, h * HALF : (h + 1) * HALF], op0=ALU.mult, op1=ALU.add,
+                )
             nc.sync.dma_start(out=o0_view[i // RT][:, i % RT, :], in_=y[:])
             y_sb[i] = y
 
@@ -259,7 +265,11 @@ def tile_moietransformerblock_pb_kernel(tc, in_proto, pt_w, pln_g, pln_b, proto_
                 o8 = opool.tile([P, 4, D], FP8, name="o8", tag="o8")
                 o_sb[i // 4] = o8
             o = o_sb[i // 4]
-            nc.scalar.activation(out=o[:, q, :], in_=y_sb[i][:], func=ACT.Copy, scale=Y_SCALE, saturate=False)
+            for h in (1, 0):
+                nc.scalar.activation(
+                    out=o[:, q, h * HALF : (h + 1) * HALF], in_=y_sb[i][:, h * HALF : (h + 1) * HALF],
+                    func=ACT.Copy, scale=Y_SCALE, saturate=False,
+                )
             if q == 3:
                 t0 = (i % RT) - 3
                 nc.sync.dma_start(out=o1_view[i // RT][:, t0 : t0 + 4, :], in_=o[:].bitcast(U8))
@@ -268,45 +278,50 @@ def tile_moietransformerblock_pb_kernel(tc, in_proto, pt_w, pln_g, pln_b, proto_
             return 0 <= i < NT
 
         with tc.manual_schedule():
+            warm_ps = xps.tile([P, HALF], F32, name="x0", tag="x0")
+            for j in range(N_WARM):
+                dummy()
             for s in range(FIRST, NT + 1):
                 for need, order, kind, k in loads:
                     if need - AHEAD == s or (s == FIRST and need - AHEAD < FIRST):
                         issue_load(kind, k)
-                i1 = s + 1
-                ia = s + 3
-                iw = s + 9
-                if ok(i1):
-                    matmuls(i1)
-                if ok(ia):
-                    transpose_a(ia)
-                if ok(iw):
-                    transpose_w(iw)
+                if ok(s + 1):
+                    matmuls(s + 1, 0)
                 if ok(s):
                     std(s)
-                if ok(i1):
-                    row_sum(i1)
+                if ok(s + 1):
+                    row_sum(s + 1)
                 if ok(s - 1):
                     scale_add(s - 1)
-                if ok(ia):
-                    copy_a(ia)
-                if ok(i1):
-                    half_mean(i1)
-                if ok(iw):
-                    copy_w(iw)
-                if ok(i1):
-                    half_m2(i1)
-                if ok(s):
-                    centre_gain(s)
-                    rstd(s)
-                if ok(i1):
-                    bn(i1)
-                if ok(ia):
-                    quant_a(ia)
-                if ok(iw):
-                    quant_w(iw)
-                if ok(i1):
-                    aggr(i1)
-                if ok(s - 1):
                     cast(s - 1)
-                if ok(i1):
-                    resid(i1)
+                if ok(s + 4):
+                    transpose_a(s + 4)
+                if ok(s):
+                    centre_gain(s, 1)
+                if ok(s + 2):
+                    matmuls(s + 2, 1)
+                if ok(s + 1):
+                    half_mean(s + 1)
+                if ok(s + 4):
+                    copy_a(s + 4)
+                if ok(s + 3):
+                    quant_a(s + 3)
+                if ok(s + 10):
+                    quant_w(s + 10)
+                if ok(s):
+                    rstd(s)
+                if ok(s + 11):
+                    transpose_w(s + 11)
+                if s < -2:
+                    dummy()
+                if ok(s + 1):
+                    half_m2(s + 1)
+                if ok(s + 11):
+                    copy_w(s + 11)
+                if ok(s + 1):
+                    bn(s + 1)
+                if ok(s):
+                    centre_gain(s, 0)
+                if ok(s + 1):
+                    aggr(s + 1)
+                    resid(s + 1)

@@ -24,7 +24,8 @@ HALF = 512
 LN_EPS = 1e-5
 Y_SCALE = 190.0
 AHEAD = 6
-FIRST = -11
+FIRST = -12
+CG = 768
 N_WARM = 8
 HEAD_W = 8
 
@@ -42,14 +43,16 @@ def tile_moietransformerblock_pb_kernel(tc, in_proto, pt_w, pln_g, pln_b, proto_
         raw = ctx.enter_context(tc.tile_pool(name="raw", bufs=6))
         grp = ctx.enter_context(tc.tile_pool(name="grp", bufs=3))
         acode = ctx.enter_context(tc.tile_pool(name="acode", bufs=4))
-        wcode = ctx.enter_context(tc.tile_pool(name="wcode", bufs=2))
+        wcode = ctx.enter_context(tc.tile_pool(name="wcode", bufs=3))
         small = ctx.enter_context(tc.tile_pool(name="small", bufs=4))
         tpool = ctx.enter_context(tc.tile_pool(name="tpool", bufs=2))
-        cpool = ctx.enter_context(tc.tile_pool(name="cpool", bufs=3))
+        cgpool = ctx.enter_context(tc.tile_pool(name="cgpool", bufs=2))
+        cvpool = ctx.enter_context(tc.tile_pool(name="cvpool", bufs=3))
         ypool = ctx.enter_context(tc.tile_pool(name="ypool", bufs=4))
         opool = ctx.enter_context(tc.tile_pool(name="opool", bufs=2))
         xps = ctx.enter_context(tc.psum_pool(name="xps", bufs=2))
-        tps = ctx.enter_context(tc.psum_pool(name="tps", bufs=4))
+        tps = ctx.enter_context(tc.psum_pool(name="tps", bufs=3))
+        jps = ctx.enter_context(tc.psum_pool(name="jps", bufs=1))
 
         ident = const.tile([P, P], F32, name="ident")
         make_identity(nc, ident[:])
@@ -60,6 +63,12 @@ def tile_moietransformerblock_pb_kernel(tc, in_proto, pt_w, pln_g, pln_b, proto_
         st = [const.tile([P, 9], F32, name="st%d" % j) for j in range(2)]
         for j in range(2):
             nc.vector.memset(st[j][:, 6:7], float(HALF))
+        identb = const.tile([P, P], BF16, name="identb")
+        make_identity(nc, identb[:])
+        rows = const.tile([P, D], BF16, name="rows")
+        nc.vector.memset(rows[:], 0.0)
+        nc.sync.dma_start(out=rows[0:NB, :], in_=pln_g)
+        nc.sync.dma_start(out=rows[NB : 2 * NB, :], in_=pln_b)
         zeros = const.tile([P, HALF], BF16, name="zeros")
         nc.vector.memset(zeros[:], 0.0)
         gain = const.tile([P, NB, D], BF16, name="gain")
@@ -82,18 +91,16 @@ def tile_moietransformerblock_pb_kernel(tc, in_proto, pt_w, pln_g, pln_b, proto_
         sd = {}
         rs = {}
         t_sb = {}
-        c_sb = {}
+        cg_sb = {}
+        cv_sb = {}
         y_sb = {}
         o_sb = {}
 
         loads = []
         for k in range(NT // 2):
-            loads.append((2 * k - 11, 0, "w", k))
-            loads.append((2 * k - 4, 1, "a", k))
-            loads.append((2 * k - 1, 2, "r", k))
-        for n in range(NB):
-            loads.append((RT * n - 1, 3, "b", n))
-            loads.append((RT * n, 4, "g", n))
+            loads.append((2 * k - 12, 3, "w", k))
+            loads.append((2 * k - 4, 0, "a", k))
+            loads.append((2 * k - 1, 4, "r", k))
         loads = sorted(loads)
 
         def issue_load(kind, k):
@@ -107,14 +114,10 @@ def tile_moietransformerblock_pb_kernel(tc, in_proto, pt_w, pln_g, pln_b, proto_
                 ar = raw.tile([P, 2, K], BF16, name="ar", tag="ar")
                 nc.sync.dma_start(out=ar[:], in_=a_view[n][:, 2 * c : 2 * c + 2, :])
                 araw[k] = ar
-            elif kind == "r":
+            else:
                 rr = raw.tile([P, 2, D], BF16, name="rr", tag="rr")
                 nc.sync.dma_start(out=rr[:], in_=r_view[n][:, 2 * c : 2 * c + 2, :])
                 rraw[k] = rr
-            elif kind == "b":
-                nc.sync.dma_start(out=beta[:, k, :], in_=pln_b[k].partition_broadcast(P))
-            else:
-                nc.sync.dma_start(out=gain[:, k, :], in_=pln_g[k].partition_broadcast(P))
 
         def transposes(src, dst):
             words = src.bitcast(F32)
@@ -193,7 +196,35 @@ def tile_moietransformerblock_pb_kernel(tc, in_proto, pt_w, pln_g, pln_b, proto_
                 )
 
         def dummy():
-            nc.tensor.matmul(out=warm_ps[:], lhsT=zeros[:, 0:P], rhs=zeros[:], start=True, stop=True)
+            nc.tensor.matmul(out=junk_ps[:], lhsT=zeros[:, 0:P], rhs=zeros[:], start=True, stop=True)
+
+        def spread(idx):
+            n = idx // 4
+            which = (idx % 4) // 2
+            h = idx % 2
+            row = which * NB + n
+            ps = xps.tile([P, HALF], F32, name="x%d" % h, tag="x%d" % h)
+            nc.tensor.matmul(
+                out=ps[:], lhsT=identb[:, row : row + 1].to_broadcast([P, P]),
+                rhs=rows[:, h * HALF : (h + 1) * HALF], start=True, stop=True,
+            )
+            dst = (gain if which == 0 else beta)[:, n, h * HALF : (h + 1) * HALF]
+            if h == 0:
+                nc.vector.tensor_copy(out=dst, in_=ps[:])
+            else:
+                nc.scalar.copy(out=dst, in_=ps[:])
+
+        def dummy_mx(i):
+            n = i // RT
+            nc.tensor.matmul_mx(
+                out=junk_ps[:],
+                lhsT=a_c[i][:, 0:P].bitcast(FP8X4),
+                lhsT_scale=a_s[i][:, 0:P],
+                rhs=w_c[n][:, 0, 0:HALF].bitcast(FP8X4),
+                rhs_scale=w_s[n][:, 0, 0:HALF],
+                start=True,
+                stop=True,
+            )
 
         def row_sum(i):
             sm = small.tile([P, 1], F32, name="sm", tag="sm")
@@ -239,23 +270,28 @@ def tile_moietransformerblock_pb_kernel(tc, in_proto, pt_w, pln_g, pln_b, proto_
                 in1=gain[:, n, h * HALF : (h + 1) * HALF], op0=ALU.subtract, op1=ALU.mult,
             )
 
-        def resid(i):
-            n = i // RT
-            c = cpool.tile([P, D], F32, name="c", tag="c")
-            for h in range(2):
-                nc.gpsimd.tensor_tensor(
-                    out=c[:, h * HALF : (h + 1) * HALF], in0=rraw[i // 2][:, i % 2, h * HALF : (h + 1) * HALF],
-                    in1=beta[:, n, h * HALF : (h + 1) * HALF], op=ALU.add,
-                )
-            c_sb[i] = c
+        def resid_g(i):
+            cg = cgpool.tile([P, CG], F32, name="cg", tag="cg")
+            nc.gpsimd.tensor_tensor(
+                out=cg[:], in0=rraw[i // 2][:, i % 2, 0:CG], in1=beta[:, i // RT, 0:CG], op=ALU.add,
+            )
+            cg_sb[i] = cg
+
+        def resid_v(i):
+            cv = cvpool.tile([P, D - CG], F32, name="cv", tag="cv")
+            nc.vector.tensor_tensor(
+                out=cv[:], in0=rraw[i // 2][:, i % 2, CG:D], in1=beta[:, i // RT, CG:D], op=ALU.add,
+            )
+            cv_sb[i] = cv
 
         def scale_add(i):
             y = ypool.tile([P, D], F32, name="y", tag="y")
-            for h in (1, 0):
-                nc.vector.scalar_tensor_tensor(
-                    out=y[:, h * HALF : (h + 1) * HALF], in0=t_sb[i][:, h * HALF : (h + 1) * HALF], scalar=rs[i][:],
-                    in1=c_sb[i][:, h * HALF : (h + 1) * HALF], op0=ALU.mult, op1=ALU.add,
-                )
+            nc.vector.scalar_tensor_tensor(
+                out=y[:, CG:D], in0=t_sb[i][:, CG:D], scalar=rs[i][:], in1=cv_sb[i][:], op0=ALU.mult, op1=ALU.add,
+            )
+            nc.vector.scalar_tensor_tensor(
+                out=y[:, 0:CG], in0=t_sb[i][:, 0:CG], scalar=rs[i][:], in1=cg_sb[i][:], op0=ALU.mult, op1=ALU.add,
+            )
             nc.sync.dma_start(out=o0_view[i // RT][:, i % RT, :], in_=y[:])
             y_sb[i] = y
 
@@ -265,11 +301,7 @@ def tile_moietransformerblock_pb_kernel(tc, in_proto, pt_w, pln_g, pln_b, proto_
                 o8 = opool.tile([P, 4, D], FP8, name="o8", tag="o8")
                 o_sb[i // 4] = o8
             o = o_sb[i // 4]
-            for h in (1, 0):
-                nc.scalar.activation(
-                    out=o[:, q, h * HALF : (h + 1) * HALF], in_=y_sb[i][:, h * HALF : (h + 1) * HALF],
-                    func=ACT.Copy, scale=Y_SCALE, saturate=False,
-                )
+            nc.scalar.activation(out=o[:, q, :], in_=y_sb[i][:], func=ACT.Copy, scale=Y_SCALE, saturate=False)
             if q == 3:
                 t0 = (i % RT) - 3
                 nc.sync.dma_start(out=o1_view[i // RT][:, t0 : t0 + 4, :], in_=o[:].bitcast(U8))
@@ -278,9 +310,11 @@ def tile_moietransformerblock_pb_kernel(tc, in_proto, pt_w, pln_g, pln_b, proto_
             return 0 <= i < NT
 
         with tc.manual_schedule():
-            warm_ps = xps.tile([P, HALF], F32, name="x0", tag="x0")
+            junk_ps = jps.tile([P, HALF], F32, name="junk_ps")
             for j in range(N_WARM):
                 dummy()
+            for idx in range(4):
+                spread(idx)
             for s in range(FIRST, NT + 1):
                 for need, order, kind, k in loads:
                     if need - AHEAD == s or (s == FIRST and need - AHEAD < FIRST):
@@ -291,37 +325,45 @@ def tile_moietransformerblock_pb_kernel(tc, in_proto, pt_w, pln_g, pln_b, proto_
                     std(s)
                 if ok(s + 1):
                     row_sum(s + 1)
-                if ok(s - 1):
-                    scale_add(s - 1)
-                    cast(s - 1)
-                if ok(s + 4):
-                    transpose_a(s + 4)
-                if ok(s):
-                    centre_gain(s, 1)
-                if ok(s + 2):
-                    matmuls(s + 2, 1)
-                if ok(s + 1):
                     half_mean(s + 1)
-                if ok(s + 4):
-                    copy_a(s + 4)
                 if ok(s + 3):
                     quant_a(s + 3)
                 if ok(s + 10):
                     quant_w(s + 10)
-                if ok(s):
-                    rstd(s)
-                if ok(s + 11):
-                    transpose_w(s + 11)
-                if s < -2:
-                    dummy()
                 if ok(s + 1):
-                    half_m2(s + 1)
+                    resid_v(s + 1)
+                if ok(s - 1):
+                    scale_add(s - 1)
+                if ok(s + 1):
+                    resid_g(s + 1)
+                if ok(s + 4):
+                    transpose_a(s + 4)
+                if ok(s + 1):
+                    dummy_mx(s + 1)
                 if ok(s + 11):
                     copy_w(s + 11)
                 if ok(s + 1):
+                    half_m2(s + 1)
+                if ok(s + 4):
+                    copy_a(s + 4)
+                if ok(s - 1):
+                    cast(s - 1)
+                if ok(s):
+                    centre_gain(s, 1)
+                if ok(s + 2):
+                    matmuls(s + 2, 1)
+                if ok(s + 12):
+                    transpose_w(s + 12)
+                if ok(s + 2):
+                    dummy_mx(s + 2)
+                if s < -4:
+                    spread(4 + s - FIRST)
+                elif s < -2:
+                    dummy()
+                if ok(s + 1):
                     bn(s + 1)
                 if ok(s):
+                    rstd(s)
                     centre_gain(s, 0)
                 if ok(s + 1):
                     aggr(s + 1)
-                    resid(s + 1)

@@ -26,7 +26,7 @@ Y_SCALE = 190.0
 AHEAD = 6
 FIRST = -12
 CG = 768
-N_WARM = 8
+N_WARM = 6
 HEAD_W = 8
 
 
@@ -47,30 +47,29 @@ def tile_moietransformerblock_pb_kernel(tc, in_proto, pt_w, pln_g, pln_b, proto_
         small = ctx.enter_context(tc.tile_pool(name="small", bufs=4))
         tpool = ctx.enter_context(tc.tile_pool(name="tpool", bufs=2))
         cgpool = ctx.enter_context(tc.tile_pool(name="cgpool", bufs=2))
-        cvpool = ctx.enter_context(tc.tile_pool(name="cvpool", bufs=3))
         ypool = ctx.enter_context(tc.tile_pool(name="ypool", bufs=4))
         opool = ctx.enter_context(tc.tile_pool(name="opool", bufs=2))
         xps = ctx.enter_context(tc.psum_pool(name="xps", bufs=2))
         tps = ctx.enter_context(tc.psum_pool(name="tps", bufs=3))
-        jps = ctx.enter_context(tc.psum_pool(name="jps", bufs=1))
+        cps = ctx.enter_context(tc.psum_pool(name="cps", bufs=1))
 
+        zeros = const.tile([P, P], F32, name="zeros")
+        nc.vector.memset(zeros[:], 0.0)
+        rows = const.tile([P, D], BF16, name="rows")
+        nc.vector.memset(rows[:], 0.0)
+        nc.sync.dma_start(out=rows[0:NB, :], in_=pln_g)
+        nc.sync.dma_start(out=rows[NB : 2 * NB, :], in_=pln_b)
         ident = const.tile([P, P], F32, name="ident")
         make_identity(nc, ident[:])
         eps = const.tile([P, 1], F32, name="eps")
         nc.vector.memset(eps[:], LN_EPS)
         warm = const.tile([P, 1], F32, name="warm")
-        nc.scalar.activation(out=warm[:], in_=eps[:], func=ACT.Sqrt, bias=eps[:], scale=1.0)
+        nc.scalar.activation(out=warm[:], in_=eps[:], func=ACT.Abs_reciprocal_sqrt, bias=eps[:], scale=1.0)
         st = [const.tile([P, 9], F32, name="st%d" % j) for j in range(2)]
         for j in range(2):
             nc.vector.memset(st[j][:, 6:7], float(HALF))
         identb = const.tile([P, P], BF16, name="identb")
         make_identity(nc, identb[:])
-        rows = const.tile([P, D], BF16, name="rows")
-        nc.vector.memset(rows[:], 0.0)
-        nc.sync.dma_start(out=rows[0:NB, :], in_=pln_g)
-        nc.sync.dma_start(out=rows[NB : 2 * NB, :], in_=pln_b)
-        zeros = const.tile([P, HALF], BF16, name="zeros")
-        nc.vector.memset(zeros[:], 0.0)
         gain = const.tile([P, NB, D], BF16, name="gain")
         beta = const.tile([P, NB, D], BF16, name="beta")
 
@@ -92,6 +91,7 @@ def tile_moietransformerblock_pb_kernel(tc, in_proto, pt_w, pln_g, pln_b, proto_
         rs = {}
         t_sb = {}
         cg_sb = {}
+        sp_ps = {}
         cv_sb = {}
         y_sb = {}
         o_sb = {}
@@ -140,8 +140,7 @@ def tile_moietransformerblock_pb_kernel(tc, in_proto, pt_w, pln_g, pln_b, proto_
             transposes(wraw[w // 2][:, w % 2, :], tp)
             tp_w[w] = tp
 
-        def interleave(on_vector, tp, gt):
-            dst = gt[:].bitcast(F32).rearrange("p (g r u) -> p g r u", g=2, u=2)
+        def interleave(on_vector, tp, dst):
             src = tp[:].rearrange("p (g u r) -> p g r u", g=2, u=2)
             if on_vector:
                 nc.vector.tensor_copy(out=dst, in_=src)
@@ -150,13 +149,15 @@ def tile_moietransformerblock_pb_kernel(tc, in_proto, pt_w, pln_g, pln_b, proto_
 
         def copy_a(i):
             ga = grp.tile([P, K], BF16, name="ga", tag="ga", align_bytes=64)
-            interleave(False, tp_a[i], ga)
             g_a[i] = ga
+            interleave(False, tp_a[i], ga[:].bitcast(F32).rearrange("p (g r u) -> p g r u", g=2, u=2))
 
         def copy_w(w):
-            gw = grp.tile([P, K], BF16, name="gw", tag="gw", align_bytes=64)
-            interleave(w < HEAD_W and w % 2 == 1, tp_w[w], gw)
-            g_w[w] = gw
+            if w % 2 == 0:
+                gw = grp.tile([P, 2, 2, HALF], BF16, name="gw", tag="gw", align_bytes=64)
+                g_w[w // 2] = gw
+            dst = g_w[w // 2][:, :, w % 2, :].bitcast(F32).rearrange("p g (r u) -> p g r u", u=2)
+            interleave(w < HEAD_W and w % 2 == 1, tp_w[w], dst)
 
         def quant_a(i):
             ac = acode.tile([P, 2 * P], U32, name="ac", tag="ac", align_bytes=64)
@@ -165,19 +166,19 @@ def tile_moietransformerblock_pb_kernel(tc, in_proto, pt_w, pln_g, pln_b, proto_
             a_c[i] = ac
             a_s[i] = asc
 
-        def quant_w(w):
-            n = w // RT
-            j = w % RT
-            if j == 0:
+        def quant_w(pair):
+            n = pair // 4
+            j0 = 2 * (pair % 4)
+            if j0 == 0:
                 wc = wcode.tile([P, 2, D], U32, name="wc", tag="wc", align_bytes=64)
                 wsc = wcode.tile([P, 2, D], U8, name="wsc", tag="wsc", align_bytes=64)
                 w_c[n] = wc
                 w_s[n] = wsc
             for g in range(2):
                 nc.vector.quantize_mx(
-                    out=w_c[n][:, g, j * P : (j + 1) * P].bitcast(FP8X4),
-                    scales=w_s[n][:, g, j * P : (j + 1) * P],
-                    in_=g_w[w][:, g * HALF : (g + 1) * HALF],
+                    out=w_c[n][:, g, j0 * P : (j0 + 2) * P].bitcast(FP8X4),
+                    scales=w_s[n][:, g, j0 * P : (j0 + 2) * P],
+                    in_=g_w[pair][:, g, :, :].rearrange("p j c -> p (j c)"),
                 )
 
         def matmuls(i, h):
@@ -195,50 +196,39 @@ def tile_moietransformerblock_pb_kernel(tc, in_proto, pt_w, pln_g, pln_b, proto_
                     stop=(g == 1),
                 )
 
-        def dummy():
-            nc.tensor.matmul(out=junk_ps[:], lhsT=zeros[:, 0:P], rhs=zeros[:], start=True, stop=True)
-
         def spread(idx):
-            n = idx // 4
-            which = (idx % 4) // 2
+            v = idx // 2
             h = idx % 2
+            n = v // 2
+            which = 1 - v % 2
             row = which * NB + n
-            ps = xps.tile([P, HALF], F32, name="x%d" % h, tag="x%d" % h)
+            if h == 0:
+                sp = xps.tile([P, D], BF16, name="x%d" % which, tag="x%d" % which)
+                sp_ps[v] = sp
             nc.tensor.matmul(
-                out=ps[:], lhsT=identb[:, row : row + 1].to_broadcast([P, P]),
+                out=sp_ps[v][:, h * HALF : (h + 1) * HALF], lhsT=identb[:, row : row + 1].to_broadcast([P, P]),
                 rhs=rows[:, h * HALF : (h + 1) * HALF], start=True, stop=True,
             )
-            dst = (gain if which == 0 else beta)[:, n, h * HALF : (h + 1) * HALF]
-            if h == 0:
-                nc.vector.tensor_copy(out=dst, in_=ps[:])
-            else:
-                nc.scalar.copy(out=dst, in_=ps[:])
+            if h == 1:
+                if which == 0:
+                    nc.vector.tensor_copy(out=gain[:, n, :], in_=sp_ps[v][:])
+                else:
+                    nc.scalar.copy(out=beta[:, n, :], in_=sp_ps[v][:])
 
-        def dummy_mx(i):
-            n = i // RT
-            nc.tensor.matmul_mx(
-                out=junk_ps[:],
-                lhsT=a_c[i][:, 0:P].bitcast(FP8X4),
-                lhsT_scale=a_s[i][:, 0:P],
-                rhs=w_c[n][:, 0, 0:HALF].bitcast(FP8X4),
-                rhs_scale=w_s[n][:, 0, 0:HALF],
-                start=True,
-                stop=True,
-            )
+        def dummy():
+            jp = cps.tile([P, P], F32, name="cp", tag="cp")
+            nc.tensor.matmul(out=jp[:], lhsT=zeros[:], rhs=zeros[:], start=True, stop=True)
 
-        def row_sum(i):
-            sm = small.tile([P, 1], F32, name="sm", tag="sm")
-            junk = small.tile([P, HALF], BF16, name="junk", tag="junk")
-            nc.scalar.activation(out=junk[:], in_=x_ps[(i, 1)][:], func=ACT.Copy, accum_out=sm[:])
-            sums[i] = sm
-
-        def half_mean(i):
-            nc.scalar.activation(out=st[i % 2][:, 7:8], in_=sums[i][:], func=ACT.Copy, scale=1.0 / HALF)
-
-        def half_m2(i):
+        def half_mean(i, h):
             junk = small.tile([P, HALF], BF16, name="junk", tag="junk")
             nc.scalar.activation(
-                out=junk[:], in_=x_ps[(i, 1)][:], func=ACT.Square, scale=-1.0,
+                out=junk[:], in_=x_ps[(i, h)][:], func=ACT.Copy, scale=1.0 / HALF, accum_out=st[i % 2][:, 7:8],
+            )
+
+        def half_m2(i, h):
+            junk = small.tile([P, HALF], BF16, name="junk", tag="junk")
+            nc.scalar.activation(
+                out=junk[:], in_=x_ps[(i, h)][:], func=ACT.Square, scale=-1.0,
                 bias=st[i % 2][:, 7:8], accum_out=st[i % 2][:, 8:9],
             )
 
@@ -250,14 +240,9 @@ def tile_moietransformerblock_pb_kernel(tc, in_proto, pt_w, pln_g, pln_b, proto_
             nc.vector.bn_aggr(out=m[:], in_=st[i % 2][:])
             mv[i] = m
 
-        def std(i):
-            sdev = small.tile([P, 1], F32, name="sdev", tag="sdev")
-            nc.scalar.activation(out=sdev[:], in_=mv[i][:, 1:2], func=ACT.Sqrt, bias=eps[:], scale=1.0)
-            sd[i] = sdev
-
         def rstd(i):
             r = small.tile([P, 1], F32, name="r", tag="r")
-            nc.vector.reciprocal(out=r[:], in_=sd[i][:])
+            nc.scalar.activation(out=r[:], in_=mv[i][:, 1:2], func=ACT.Abs_reciprocal_sqrt, bias=eps[:], scale=1.0)
             rs[i] = r
 
         def centre_gain(i, h):
@@ -277,23 +262,29 @@ def tile_moietransformerblock_pb_kernel(tc, in_proto, pt_w, pln_g, pln_b, proto_
             )
             cg_sb[i] = cg
 
-        def resid_v(i):
-            cv = cvpool.tile([P, D - CG], F32, name="cv", tag="cv")
-            nc.vector.tensor_tensor(
-                out=cv[:], in0=rraw[i // 2][:, i % 2, CG:D], in1=beta[:, i // RT, CG:D], op=ALU.add,
+        def resid_pe(i):
+            row = NB + i // RT
+            cp = cps.tile([P, D - CG], F32, name="cp", tag="cp")
+            nc.tensor.matmul(out=cp[:], lhsT=identb[:], rhs=rraw[i // 2][:, i % 2, CG:D], start=True, stop=False)
+            nc.tensor.matmul(
+                out=cp[:], lhsT=identb[:, row : row + 1].to_broadcast([P, P]), rhs=rows[:, CG:D],
+                start=False, stop=True,
             )
-            cv_sb[i] = cv
+            cv_sb[i] = cp
 
-        def scale_add(i):
+        def scale_add_g(i):
             y = ypool.tile([P, D], F32, name="y", tag="y")
-            nc.vector.scalar_tensor_tensor(
-                out=y[:, CG:D], in0=t_sb[i][:, CG:D], scalar=rs[i][:], in1=cv_sb[i][:], op0=ALU.mult, op1=ALU.add,
-            )
             nc.vector.scalar_tensor_tensor(
                 out=y[:, 0:CG], in0=t_sb[i][:, 0:CG], scalar=rs[i][:], in1=cg_sb[i][:], op0=ALU.mult, op1=ALU.add,
             )
-            nc.sync.dma_start(out=o0_view[i // RT][:, i % RT, :], in_=y[:])
             y_sb[i] = y
+
+        def scale_add_p(i):
+            y = y_sb[i]
+            nc.vector.scalar_tensor_tensor(
+                out=y[:, CG:D], in0=t_sb[i][:, CG:D], scalar=rs[i][:], in1=cv_sb[i][:], op0=ALU.mult, op1=ALU.add,
+            )
+            nc.sync.dma_start(out=o0_view[i // RT][:, i % RT, :], in_=y[:])
 
         def cast(i):
             q = i % 4
@@ -302,48 +293,47 @@ def tile_moietransformerblock_pb_kernel(tc, in_proto, pt_w, pln_g, pln_b, proto_
                 o_sb[i // 4] = o8
             o = o_sb[i // 4]
             nc.scalar.activation(out=o[:, q, :], in_=y_sb[i][:], func=ACT.Copy, scale=Y_SCALE, saturate=False)
-            if q == 3:
-                t0 = (i % RT) - 3
+            t0 = (i % RT) - q
+            if i == NT - 2:
+                nc.sync.dma_start(out=o1_view[i // RT][:, t0 : t0 + 3, :], in_=o[:, 0:3, :].bitcast(U8))
+            elif i == NT - 1:
+                nc.sync.dma_start(out=o1_view[i // RT][:, t0 + 3, :], in_=o[:, 3, :].bitcast(U8))
+            elif q == 3:
                 nc.sync.dma_start(out=o1_view[i // RT][:, t0 : t0 + 4, :], in_=o[:].bitcast(U8))
 
         def ok(i):
             return 0 <= i < NT
 
         with tc.manual_schedule():
-            junk_ps = jps.tile([P, HALF], F32, name="junk_ps")
             for j in range(N_WARM):
                 dummy()
-            for idx in range(4):
-                spread(idx)
             for s in range(FIRST, NT + 1):
                 for need, order, kind, k in loads:
                     if need - AHEAD == s or (s == FIRST and need - AHEAD < FIRST):
                         issue_load(kind, k)
                 if ok(s + 1):
                     matmuls(s + 1, 0)
+                    half_mean(s + 1, 1)
                 if ok(s):
-                    std(s)
-                if ok(s + 1):
-                    row_sum(s + 1)
-                    half_mean(s + 1)
+                    rstd(s)
                 if ok(s + 3):
                     quant_a(s + 3)
-                if ok(s + 10):
-                    quant_w(s + 10)
-                if ok(s + 1):
-                    resid_v(s + 1)
+                if ok(s + 10) and (s + 10) % 2 == 1:
+                    quant_w((s + 10) // 2)
                 if ok(s - 1):
-                    scale_add(s - 1)
+                    scale_add_g(s - 1)
                 if ok(s + 1):
                     resid_g(s + 1)
+                if ok(s - 1):
+                    scale_add_p(s - 1)
                 if ok(s + 4):
                     transpose_a(s + 4)
-                if ok(s + 1):
-                    dummy_mx(s + 1)
+                if ok(s):
+                    resid_pe(s)
                 if ok(s + 11):
                     copy_w(s + 11)
                 if ok(s + 1):
-                    half_m2(s + 1)
+                    half_m2(s + 1, 1)
                 if ok(s + 4):
                     copy_a(s + 4)
                 if ok(s - 1):
@@ -354,16 +344,14 @@ def tile_moietransformerblock_pb_kernel(tc, in_proto, pt_w, pln_g, pln_b, proto_
                     matmuls(s + 2, 1)
                 if ok(s + 12):
                     transpose_w(s + 12)
-                if ok(s + 2):
-                    dummy_mx(s + 2)
                 if s < -4:
-                    spread(4 + s - FIRST)
+                    spread(s - FIRST)
                 elif s < -2:
-                    dummy()
+                    spread(2 * s + 16)
+                    spread(2 * s + 17)
                 if ok(s + 1):
                     bn(s + 1)
                 if ok(s):
-                    rstd(s)
                     centre_gain(s, 0)
                 if ok(s + 1):
                     aggr(s + 1)

@@ -328,6 +328,8 @@ def tile_moietransformerblock_pb_kernel(tc, in_proto, pt_w, pln_g, pln_b, proto_
                     scale_add_p(s - 1)
                 if ok(s + 4):
                     transpose_a(s + 4)
+                if ok(s + 12) and s >= -1:
+                    transpose_w(s + 12)
                 if ok(s):
                     resid_pe(s)
                 if ok(s + 11):
@@ -342,7 +344,7 @@ def tile_moietransformerblock_pb_kernel(tc, in_proto, pt_w, pln_g, pln_b, proto_
                     centre_gain(s, 1)
                 if ok(s + 2):
                     matmuls(s + 2, 1)
-                if ok(s + 12):
+                if ok(s + 12) and s < -1:
                     transpose_w(s + 12)
                 if s < -4:
                     spread(s - FIRST)

from contextlib import ExitStack

import concourse.mybir as mybir
from concourse.masks import make_identity

FLOPS = 2 * 3 * 1024 * 1024 * 1024

F32 = mybir.dt.float32
BF16 = mybir.dt.bfloat16
U32 = mybir.dt.uint32
U8 = mybir.dt.uint8
FP8X4 = mybir.dt.float8_e4m3fn_x4
FP8 = mybir.dt.float8_e4m3fn
ACT = mybir.ActivationFunctionType
ALU = mybir.AluOpType

P = 128
NB = 3
RT = 8
NT = NB * RT
K = 1024
D = 1024
HALF = 512
LN_EPS = 1e-5
Y_SCALE = 190.0
AHEAD = 6
FIRST = -12
CG = 768
N_WARM = 6
HEAD_W = 8


def tile_moietransformerblock_pb_kernel(tc, in_proto, pt_w, pln_g, pln_b, proto_w, out_0, out_1):
    nc = tc.nc
    a_view = [in_proto[n].rearrange("(p t) k -> p t k", t=RT) for n in range(NB)]
    w_view = [pt_w[n].rearrange("(t p) k -> p t k", p=P) for n in range(NB)]
    r_view = [proto_w[n].rearrange("(p t) d -> p t d", t=RT) for n in range(NB)]
    o0_view = [out_0[n].rearrange("(p t) d -> p t d", t=RT) for n in range(NB)]
    o1_view = [out_1[n].rearrange("(p t) d -> p t d", t=RT) for n in range(NB)]

    with ExitStack() as ctx:
        const = ctx.enter_context(tc.tile_pool(name="const", bufs=1))
        raw = ctx.enter_context(tc.tile_pool(name="raw", bufs=6))
        grp = ctx.enter_context(tc.tile_pool(name="grp", bufs=3))
        acode = ctx.enter_context(tc.tile_pool(name="acode", bufs=4))
        wcode = ctx.enter_context(tc.tile_pool(name="wcode", bufs=3))
        small = ctx.enter_context(tc.tile_pool(name="small", bufs=4))
        tpool = ctx.enter_context(tc.tile_pool(name="tpool", bufs=2))
        cgpool = ctx.enter_context(tc.tile_pool(name="cgpool", bufs=2))
        ypool = ctx.enter_context(tc.tile_pool(name="ypool", bufs=4))
        opool = ctx.enter_context(tc.tile_pool(name="opool", bufs=2))
        xps = ctx.enter_context(tc.psum_pool(name="xps", bufs=2))
        tps = ctx.enter_context(tc.psum_pool(name="tps", bufs=3))
        cps = ctx.enter_context(tc.psum_pool(name="cps", bufs=1))

        zeros = const.tile([P, P], F32, name="zeros")
        nc.vector.memset(zeros[:], 0.0)
        rows = const.tile([P, D], BF16, name="rows")
        nc.vector.memset(rows[:], 0.0)
        nc.sync.dma_start(out=rows[0:NB, :], in_=pln_g)
        nc.sync.dma_start(out=rows[NB : 2 * NB, :], in_=pln_b)
        ident = const.tile([P, P], F32, name="ident")
        make_identity(nc, ident[:])
        eps = const.tile([P, 1], F32, name="eps")
        nc.vector.memset(eps[:], LN_EPS)
        warm = const.tile([P, 1], F32, name="warm")
        nc.scalar.activation(out=warm[:], in_=eps[:], func=ACT.Abs_reciprocal_sqrt, bias=eps[:], scale=1.0)
        st = [const.tile([P, 9], F32, name="st%d" % j) for j in range(2)]
        for j in range(2):
            nc.vector.memset(st[j][:, 6:7], float(HALF))
        identb = const.tile([P, P], BF16, name="identb")
        make_identity(nc, identb[:])
        gain = const.tile([P, NB, D], BF16, name="gain")
        beta = const.tile([P, NB, D], BF16, name="beta")

        wraw = {}
        araw = {}
        rraw = {}
        tp_a = {}
        tp_w = {}
        g_a = {}
        g_w = {}
        a_c = {}
        a_s = {}
        w_c = {}
        w_s = {}
        x_ps = {}
        sums = {}
        mv = {}
        sd = {}
        rs = {}
        t_sb = {}
        cg_sb = {}
        sp_ps = {}
        cv_sb = {}
        y_sb = {}
        o_sb = {}

        loads = []
        for k in range(NT // 2):
            loads.append((2 * k - 12, 3, "w", k))
            loads.append((2 * k - 4, 0, "a", k))
            loads.append((2 * k - 1, 4, "r", k))
        loads = sorted(loads)

        def issue_load(kind, k):
            n = k // 4
            c = k % 4
            if kind == "w":
                wr = raw.tile([P, 2, K], BF16, name="wr", tag="wr")
                nc.sync.dma_start(out=wr[:], in_=w_view[n][:, 2 * c : 2 * c + 2, :])
                wraw[k] = wr
            elif kind == "a":
                ar = raw.tile([P, 2, K], BF16, name="ar", tag="ar")
                nc.sync.dma_start(out=ar[:], in_=a_view[n][:, 2 * c : 2 * c + 2, :])
                araw[k] = ar
            else:
                rr = raw.tile([P, 2, D], BF16, name="rr", tag="rr")
                nc.sync.dma_start(out=rr[:], in_=r_view[n][:, 2 * c : 2 * c + 2, :])
                rraw[k] = rr

        def transposes(src, dst):
            words = src.bitcast(F32)
            for g in range(2):
                for u in range(2):
                    q = 2 * g + u
                    nc.tensor.transpose(
                        out=dst[:, q * P : (q + 1) * P],
                        in_=words[:, 256 * g + u : 256 * (g + 1) : 2],
                        identity=ident[:],
                    )

        def transpose_a(i):
            tp = tps.tile([P, HALF], F32, name="tp", tag="tp")
            transposes(araw[i // 2][:, i % 2, :], tp)
            tp_a[i] = tp

        def transpose_w(w):
            tp = tps.tile([P, HALF], F32, name="tp", tag="tp")
            transposes(wraw[w // 2][:, w % 2, :], tp)
            tp_w[w] = tp

        def interleave(on_vector, tp, dst):
            src = tp[:].rearrange("p (g u r) -> p g r u", g=2, u=2)
            if on_vector:
                nc.vector.tensor_copy(out=dst, in_=src)
            else:
                nc.scalar.copy(out=dst, in_=src)

        def copy_a(i):
            ga = grp.tile([P, K], BF16, name="ga", tag="ga", align_bytes=64)
            g_a[i] = ga
            interleave(False, tp_a[i], ga[:].bitcast(F32).rearrange("p (g r u) -> p g r u", g=2, u=2))

        def copy_w(w):
            if w % 2 == 0:
                gw = grp.tile([P, 2, 2, HALF], BF16, name="gw", tag="gw", align_bytes=64)
                g_w[w // 2] = gw
            dst = g_w[w // 2][:, :, w % 2, :].bitcast(F32).rearrange("p g (r u) -> p g r u", u=2)
            interleave(w < HEAD_W and w % 2 == 1, tp_w[w], dst)

        def quant_a(i):
            ac = acode.tile([P, 2 * P], U32, name="ac", tag="ac", align_bytes=64)
            asc = acode.tile([P, 2 * P], U8, name="asc", tag="asc", align_bytes=64)
            nc.vector.quantize_mx(out=ac[:].bitcast(FP8X4), scales=asc[:], in_=g_a[i][:])
            a_c[i] = ac
            a_s[i] = asc

        def quant_w(pair):
            n = pair // 4
            j0 = 2 * (pair % 4)
            if j0 == 0:
                wc = wcode.tile([P, 2, D], U32, name="wc", tag="wc", align_bytes=64)
                wsc = wcode.tile([P, 2, D], U8, name="wsc", tag="wsc", align_bytes=64)
                w_c[n] = wc
                w_s[n] = wsc
            for g in range(2):
                nc.vector.quantize_mx(
                    out=w_c[n][:, g, j0 * P : (j0 + 2) * P].bitcast(FP8X4),
                    scales=w_s[n][:, g, j0 * P : (j0 + 2) * P],
                    in_=g_w[pair][:, g, :, :].rearrange("p j c -> p (j c)"),
                )

        def matmuls(i, h):
            n = i // RT
            x = xps.tile([P, HALF], F32, name="x%d" % h, tag="x%d" % h)
            x_ps[(i, h)] = x
            for g in range(2):
                nc.tensor.matmul_mx(
                    out=x[:],
                    lhsT=a_c[i][:, g * P : (g + 1) * P].bitcast(FP8X4),
                    lhsT_scale=a_s[i][:, g * P : (g + 1) * P],
                    rhs=w_c[n][:, g, h * HALF : (h + 1) * HALF].bitcast(FP8X4),
                    rhs_scale=w_s[n][:, g, h * HALF : (h + 1) * HALF],
                    start=(g == 0),
                    stop=(g == 1),
                )

        def spread(idx):
            v = idx // 2
            h = idx % 2
            n = v // 2
            which = 1 - v % 2
            row = which * NB + n
            if h == 0:
                sp = xps.tile([P, D], BF16, name="x%d" % which, tag="x%d" % which)
                sp_ps[v] = sp
            nc.tensor.matmul(
                out=sp_ps[v][:, h * HALF : (h + 1) * HALF], lhsT=identb[:, row : row + 1].to_broadcast([P, P]),
                rhs=rows[:, h * HALF : (h + 1) * HALF], start=True, stop=True,
            )
            if h == 1:
                if which == 0:
                    nc.vector.tensor_copy(out=gain[:, n, :], in_=sp_ps[v][:])
                else:
                    nc.scalar.copy(out=beta[:, n, :], in_=sp_ps[v][:])

        def dummy():
            jp = cps.tile([P, P], F32, name="cp", tag="cp")
            nc.tensor.matmul(out=jp[:], lhsT=zeros[:], rhs=zeros[:], start=True, stop=True)

        def half_mean(i, h):
            junk = small.tile([P, HALF], BF16, name="junk", tag="junk")
            nc.scalar.activation(
                out=junk[:], in_=x_ps[(i, h)][:], func=ACT.Copy, scale=1.0 / HALF, accum_out=st[i % 2][:, 7:8],
            )

        def half_m2(i, h):
            junk = small.tile([P, HALF], BF16, name="junk", tag="junk")
            nc.scalar.activation(
                out=junk[:], in_=x_ps[(i, h)][:], func=ACT.Square, scale=-1.0,
                bias=st[i % 2][:, 7:8], accum_out=st[i % 2][:, 8:9],
            )

        def bn(i):
            nc.vector.bn_stats(out=st[i % 2][:, 0:6], in_=x_ps[(i, 0)][:])

        def aggr(i):
            m = small.tile([P, 2], F32, name="m", tag="m")
            nc.vector.bn_aggr(out=m[:], in_=st[i % 2][:])
            mv[i] = m

        def rstd(i):
            r = small.tile([P, 1], F32, name="r", tag="r")
            nc.scalar.activation(out=r[:], in_=mv[i][:, 1:2], func=ACT.Abs_reciprocal_sqrt, bias=eps[:], scale=1.0)
            rs[i] = r

        def centre_gain(i, h):
            n = i // RT
            if h == 1:
                t = tpool.tile([P, D], F32, name="t", tag="t")
                t_sb[i] = t
            nc.vector.scalar_tensor_tensor(
                out=t_sb[i][:, h * HALF : (h + 1) * HALF], in0=x_ps[(i, h)][:], scalar=mv[i][:, 0:1],
                in1=gain[:, n, h * HALF : (h + 1) * HALF], op0=ALU.subtract, op1=ALU.mult,
            )

        def resid_g(i):
            cg = cgpool.tile([P, CG], F32, name="cg", tag="cg")
            nc.gpsimd.tensor_tensor(
                out=cg[:], in0=rraw[i // 2][:, i % 2, 0:CG], in1=beta[:, i // RT, 0:CG], op=ALU.add,
            )
            cg_sb[i] = cg

        def resid_pe(i):
            row = NB + i // RT
            cp = cps.tile([P, D - CG], F32, name="cp", tag="cp")
            nc.tensor.matmul(out=cp[:], lhsT=identb[:], rhs=rraw[i // 2][:, i % 2, CG:D], start=True, stop=False)
            nc.tensor.matmul(
                out=cp[:], lhsT=identb[:, row : row + 1].to_broadcast([P, P]), rhs=rows[:, CG:D],
                start=False, stop=True,
            )
            cv_sb[i] = cp

        def scale_add_g(i):
            y = ypool.tile([P, D], F32, name="y", tag="y")
            nc.vector.scalar_tensor_tensor(
                out=y[:, 0:CG], in0=t_sb[i][:, 0:CG], scalar=rs[i][:], in1=cg_sb[i][:], op0=ALU.mult, op1=ALU.add,
            )
            y_sb[i] = y

        def scale_add_p(i):
            y = y_sb[i]
            nc.vector.scalar_tensor_tensor(
                out=y[:, CG:D], in0=t_sb[i][:, CG:D], scalar=rs[i][:], in1=cv_sb[i][:], op0=ALU.mult, op1=ALU.add,
            )
            nc.sync.dma_start(out=o0_view[i // RT][:, i % RT, :], in_=y[:])

        def cast(i):
            q = i % 4
            if q == 0:
                o8 = opool.tile([P, 4, D], FP8, name="o8", tag="o8")
                o_sb[i // 4] = o8
            o = o_sb[i // 4]
            nc.scalar.activation(out=o[:, q, :], in_=y_sb[i][:], func=ACT.Copy, scale=Y_SCALE, saturate=False)
            t0 = (i % RT) - q
            if i == NT - 2:
                nc.sync.dma_start(out=o1_view[i // RT][:, t0 : t0 + 3, :], in_=o[:, 0:3, :].bitcast(U8))
            elif i == NT - 1:
                nc.sync.dma_start(out=o1_view[i // RT][:, t0 + 3, :], in_=o[:, 3, :].bitcast(U8))
            elif q == 3:
                nc.sync.dma_start(out=o1_view[i // RT][:, t0 : t0 + 4, :], in_=o[:].bitcast(U8))

        def ok(i):
            return 0 <= i < NT

        with tc.manual_schedule():
            for j in range(N_WARM):
                dummy()
            for s in range(FIRST, NT + 1):
                for need, order, kind, k in loads:
                    if need - AHEAD == s or (s == FIRST and need - AHEAD < FIRST):
                        issue_load(kind, k)
                if ok(s + 1):
                    matmuls(s + 1, 0)
                    half_mean(s + 1, 1)
                if ok(s):
                    rstd(s)
                if ok(s + 3):
                    quant_a(s + 3)
                if ok(s + 10) and (s + 10) % 2 == 1:
                    quant_w((s + 10) // 2)
                if ok(s - 1):
                    scale_add_g(s - 1)
                if ok(s + 1):
                    resid_g(s + 1)
                if ok(s - 1):
                    scale_add_p(s - 1)
                if ok(s + 4):
                    transpose_a(s + 4)
                if ok(s + 12) and s >= -1:
                    transpose_w(s + 12)
                if ok(s):
                    resid_pe(s)
                if ok(s + 11):
                    copy_w(s + 11)
                if ok(s + 1):
                    half_m2(s + 1, 1)
                if ok(s + 4):
                    copy_a(s + 4)
                if ok(s - 1):
                    cast(s - 1)
                if ok(s):
                    centre_gain(s, 1)
                if ok(s + 2):
                    matmuls(s + 2, 1)
                if ok(s + 12) and s < -1:
                    transpose_w(s + 12)
                if s < -4:
                    spread(s - FIRST)
                elif s < -2:
                    spread(2 * s + 16)
                    spread(2 * s + 17)
                if ok(s + 1):
                    bn(s + 1)
                if ok(s):
                    centre_gain(s, 0)
                if ok(s + 1):
                    aggr(s + 1)
